import numpy as np
import ml_dtypes


def mxq(x, axis, fmt="e4m3"):
    dtype, down = {"e4m3": (ml_dtypes.float8_e4m3fn, 7), "e5m2": (ml_dtypes.float8_e5m2, 14)}[fmt]
    v = np.moveaxis(np.asarray(x, np.float32).astype(ml_dtypes.bfloat16).astype(np.float64), axis, -1)
    blocks = v.reshape(v.shape[:-1] + (-1, 32))
    amax = np.abs(blocks).max(-1, keepdims=True)
    byte = np.maximum(np.where(amax > 0, np.frexp(amax)[1] - 1 + 127, 0) - down, 1)
    scale = np.exp2(byte - 127.0)
    codes = (blocks / scale).astype(np.float32).astype(dtype).astype(np.float64)
    return np.moveaxis((codes * scale).reshape(v.shape), -1, axis)


WIDE = False


def mx_kscale(k):
    if not WIDE:
        return np.ones(k)
    levels = np.array([10, -10, 5, -5, 0])
    a = np.random.permutation(np.resize(levels, k // 512 * 4)).reshape(k // 512, 4)
    idx = np.arange(k)
    return np.exp2(a[idx // 512, idx % 128 // 32])


BF16 = ml_dtypes.bfloat16


def bf(x):
    return np.asarray(x, np.float32).astype(BF16)


def f64(x):
    return np.asarray(x).astype(np.float64)


NB, DI, DO, B = 8, 16384, 128, 128
F = NB * DO
EPS = 1e-5


def setup_inputs():
    s, t = mx_kscale(DI), mx_kscale(F)
    tk = t.reshape(NB, DO)
    return {"x": bf(np.random.standard_normal((B, DI)) * s),
            "W": bf(np.random.standard_normal((NB, DI, DO)) / np.sqrt(DI) / s[None, :, None]),
            "b": bf(np.random.standard_normal((NB, DO)) * 0.5),
            "gamma": bf((1.0 + 0.2 * np.random.standard_normal((NB, DO))) * tk),
            "beta": bf(0.2 * np.random.standard_normal((NB, DO)) * tk),
            "Wf1": bf(np.random.standard_normal((F, DO)) / np.sqrt(F) / t[:, None]),
            "bf1": bf(np.random.standard_normal(DO) * 0.3)}


def reference(x, W, b, gamma, beta, Wf1, bf1):
    w2 = f64(W).transpose(1, 0, 2).reshape(DI, F)
    h = (mxq(f64(x), 1, "e4m3") @ mxq(w2, 0, "e4m3")).reshape(B, NB, DO) + f64(b)[None]
    h = np.maximum(h, 0.0)
    mean = h.mean(axis=0, keepdims=True)
    var = ((h - mean) ** 2).mean(axis=0, keepdims=True)
    h = (h - mean) * (1.0 / np.sqrt(var + EPS)) * f64(gamma)[None] + f64(beta)[None]
    fused = h.reshape(B, F)
    return np.maximum((mxq(fused, 1, "e4m3") @ mxq(f64(Wf1), 0, "e4m3")) + f64(bf1), 0.0)

@@ -1,0 +1,249 @@
+from contextlib import ExitStack
+
+import concourse.mybir as mybir
+from concourse.masks import make_identity
+
+F32 = mybir.dt.float32
+BF16 = mybir.dt.bfloat16
+U32 = mybir.dt.uint32
+U8 = mybir.dt.uint8
+FP8X4 = mybir.dt.float8_e4m3fn_x4
+ACT = mybir.ActivationFunctionType
+ALU = mybir.AluOpType
+
+P = 128
+PACK = 4
+NB, DI, DO, B = 8, 16384, 128, 128
+EPS = 1e-5
+FLOPS = 2 * B * DI * NB * DO + 2 * B * NB * DO * DO
+
+HALVES = 2
+RUNS = 64
+CLASSES = 4
+ROWS = 16
+PASSES = ROWS // PACK
+TILE_COLS = ROWS * DO
+X_CHUNK = 4096
+LOAD_CLASSES = 2
+
+
+def tile_extremeoptimizationlayer_pa_k_kernel(tc, x, W, b, gamma, beta, Wf1, bf1, out):
+    nc = tc.nc
+    with ExitStack() as ctx:
+        keep = ctx.enter_context(tc.tile_pool(name="keep", bufs=1))
+        xin = ctx.enter_context(tc.tile_pool(name="xin", bufs=4))
+        xgp = ctx.enter_context(tc.tile_pool(name="xgp", bufs=2))
+        wraw = ctx.enter_context(tc.tile_pool(name="wraw", bufs=5))
+        wgrp = ctx.enter_context(tc.tile_pool(name="wgrp", bufs=3))
+        wq = ctx.enter_context(tc.tile_pool(name="wq", bufs=3))
+        small = ctx.enter_context(tc.tile_pool(name="small", bufs=3))
+        psum_x = ctx.enter_context(tc.psum_pool(name="psum_x", bufs=4))
+        psum_acc = ctx.enter_context(tc.psum_pool(name="psum_acc", bufs=2))
+        psum_misc = ctx.enter_context(tc.psum_pool(name="psum_misc", bufs=1))
+
+        ident = keep.tile([P, P], F32)
+        make_identity(nc, ident[:])
+
+        eps_col = keep.tile([P, 1], F32)
+        nc.vector.memset(eps_col[:], EPS)
+        warm = keep.tile([P, 1], F32)
+        nc.scalar.activation(out=warm[:], in_=eps_col[:], func=ACT.Sqrt)
+
+        par_rows = keep.tile([P, P], BF16)
+        nc.vector.memset(par_rows[:], 0.0)
+        nc.scalar.dma_start(out=par_rows[0:NB, :], in_=b)
+        nc.scalar.dma_start(out=par_rows[NB : 2 * NB, :], in_=gamma)
+        nc.scalar.dma_start(out=par_rows[2 * NB : 3 * NB, :], in_=beta)
+        bias_out = keep.tile([P, DO], BF16)
+        nc.scalar.dma_start(out=bias_out[:], in_=bf1.partition_broadcast(P))
+        wf_raw = keep.tile([P, NB, DO], BF16)
+        nc.scalar.dma_start(out=wf_raw[:], in_=Wf1.rearrange("(k p) n -> p k n", p=P))
+
+        par_f32 = keep.tile([P, P], F32)
+        nc.vector.tensor_copy(out=par_f32[:], in_=par_rows[:])
+        par_ps = psum_misc.tile([P, P], F32)
+        nc.tensor.transpose(par_ps[:], par_f32[:], ident[:])
+        par = keep.tile([P, 3 * NB], F32)
+        nc.vector.tensor_copy(out=par[:], in_=par_ps[:, 0 : 3 * NB])
+
+        xs = keep.tile([P, HALVES, CLASSES, RUNS * 32], BF16)
+        chunks_per_half = DI // HALVES // X_CHUNK
+        runs_per_chunk = X_CHUNK // 128
+        for a in range(HALVES):
+            for j in range(chunks_per_half):
+                x_chunk = xin.tile([P, X_CHUNK], BF16)
+                first = (a * chunks_per_half + j) * X_CHUNK
+                nc.sync.dma_start(out=x_chunk[:], in_=x[:, first : first + X_CHUNK])
+                nc.vector.tensor_copy(
+                    out=xs[:, a, :, j * runs_per_chunk * 32 : (j + 1) * runs_per_chunk * 32].rearrange(
+                        "r c (m e) -> r c m e", e=32
+                    ),
+                    in_=x_chunk[:].rearrange("r (m c e) -> r c m e", c=CLASSES, e=32),
+                )
+
+        x_codes = keep.tile([P, HALVES * CLASSES * PASSES, B], U32, align_bytes=64)
+        x_scales = keep.tile([P, HALVES * CLASSES * PASSES, B], U8, align_bytes=64)
+        xs_words = xs[:].bitcast(F32)
+        for a in range(HALVES):
+            for c in range(CLASSES):
+                plane = xs_words[:, a, c, :].rearrange("r (p w) -> r p w", w=ROWS // 2)
+                xg = xgp.tile([P, PASSES, B, PACK], BF16, align_bytes=64)
+                xg_words = xg[:].bitcast(F32)
+                for pair in range(PASSES // 2):
+                    xt = psum_x.tile([P, 2, 2, B], F32)
+                    for s in range(2):
+                        for u in range(2):
+                            nc.tensor.transpose(
+                                xt[:, s, u, :], plane[:, :, 2 * (2 * pair + s) + u], ident[:]
+                            )
+                    nc.scalar.copy(
+                        out=xg_words[:, 2 * pair : 2 * pair + 2, :, :],
+                        in_=xt[:].rearrange("p s u r -> p s r u"),
+                    )
+                q0 = (a * CLASSES + c) * PASSES
+                nc.vector.quantize_mx(
+                    out=x_codes[:, q0 : q0 + PASSES, :].rearrange("p s r -> p (s r)").bitcast(FP8X4),
+                    scales=x_scales[:, q0 : q0 + PASSES, :].rearrange("p s r -> p (s r)"),
+                    in_=xg[:].rearrange("p s r t -> p (s r t)"),
+                )
+
+        wf_grouped = keep.tile([P, 2, DO, PACK], BF16, align_bytes=64)
+        nc.vector.tensor_copy(
+            out=wf_grouped[:], in_=wf_raw[:].rearrange("p (g t) n -> p g n t", t=PACK)
+        )
+        wf_codes = keep.tile([P, 2, DO], U32, align_bytes=64)
+        wf_scales = keep.tile([P, 2, DO], U8, align_bytes=64)
+        nc.vector.quantize_mx(
+            out=wf_codes[:].rearrange("p g n -> p (g n)").bitcast(FP8X4),
+            scales=wf_scales[:].rearrange("p g n -> p (g n)"),
+            in_=wf_grouped[:].rearrange("p g n t -> p (g n t)"),
+        )
+
+        w_loads = W.rearrange(
+            "k (a m l c h r) o -> k a l h m c (r o)", a=HALVES, m=RUNS, c=LOAD_CLASSES, h=2, r=ROWS
+        )
+        fused = keep.tile([P, 2, B, PACK], BF16, align_bytes=64)
+        f_codes = keep.tile([P, 2, B], U32, align_bytes=64)
+        f_scales = keep.tile([P, 2, B], U8, align_bytes=64)
+        half_cols = TILE_COLS // 2
+        pass_cols = TILE_COLS // PASSES
+        n_passes = HALVES * CLASSES * PASSES
+        tiles_per_branch = HALVES * CLASSES
+        n_tiles = NB * tiles_per_branch
+        loaded = {}
+        grouped = {}
+        acc = {}
+        act = {}
+        mean_var = {}
+        std = {}
+
+        def regroup(i):
+            k, rest = divmod(i, tiles_per_branch)
+            a, c = divmod(rest, CLASSES)
+            load, c_in_load = divmod(c, LOAD_CLASSES)
+            if c_in_load == 0:
+                loaded[i // LOAD_CLASSES] = wraw.tile([P, LOAD_CLASSES, TILE_COLS], BF16, name="loaded")
+                for h in range(2):
+                    nc.sync.dma_start(out=loaded[i // LOAD_CLASSES][h:P:2, :, :], in_=w_loads[k, a, load, h])
+            raw = loaded[i // LOAD_CLASSES][:, c_in_load, :]
+            grouped[i] = wgrp.tile([P, TILE_COLS], BF16, align_bytes=64, name="grouped")
+            nc.vector.tensor_copy(
+                out=grouped[i][:, 0:half_cols].rearrange("p (s c i t) -> p s c t i", s=2, i=4, t=PACK),
+                in_=raw[:, 0:half_cols].rearrange("p (s t c i) -> p s c t i", s=2, i=4, t=PACK),
+            )
+            for s in range(PASSES // 2, PASSES):
+                cols = slice(s * pass_cols, (s + 1) * pass_cols)
+                nc.scalar.copy(
+                    out=grouped[i][:, cols].rearrange("p (c i t) -> p c t i", i=4, t=PACK),
+                    in_=raw[:, cols].rearrange("p (t c i) -> p c t i", i=4, t=PACK),
+                )
+
+        def quantise_and_multiply(i):
+            k, rest = divmod(i, tiles_per_branch)
+            if rest == 0:
+                acc[k] = psum_acc.tile([P, B], F32, name="acc")
+            codes = wq.tile([P, PASSES * DO], U32, align_bytes=64)
+            scales = wq.tile([P, PASSES * DO], U8, align_bytes=64)
+            nc.vector.quantize_mx(out=codes[:].bitcast(FP8X4), scales=scales[:], in_=grouped[i][:])
+            for s in range(PASSES):
+                q = rest * PASSES + s
+                nc.tensor.matmul_mx(
+                    out=acc[k][:],
+                    lhsT=codes[:, s * DO : (s + 1) * DO].bitcast(FP8X4),
+                    lhsT_scale=scales[:, s * DO : (s + 1) * DO],
+                    rhs=x_codes[:, q, :].bitcast(FP8X4),
+                    rhs_scale=x_scales[:, q, :],
+                    start=(q == 0),
+                    stop=(q == n_passes - 1),
+                )
+
+        def norm_relu(k):
+            act[k] = small.tile([P, B], F32, name="act")
+            nc.scalar.activation(out=act[k][:], in_=acc[k][:], func=ACT.Relu, bias=par[:, k : k + 1])
+
+        def norm_stats(k):
+            stats = small.tile([P, 6], F32)
+            nc.vector.bn_stats(out=stats[:], in_=act[k][:])
+            mean_var[k] = small.tile([P, 2], F32, name="mean_var")
+            nc.vector.bn_aggr(out=mean_var[k][:], in_=stats[:])
+
+        def norm_sqrt(k):
+            std[k] = small.tile([P, 1], F32, name="std")
+            nc.scalar.activation(out=std[k][:], in_=mean_var[k][:, 1:2], func=ACT.Sqrt, bias=eps_col[:])
+
+        def norm_apply(k):
+            rstd = small.tile([P, 1], F32)
+            nc.vector.reciprocal(out=rstd[:], in_=std[k][:])
+            gain = small.tile([P, 1], F32)
+            nc.vector.tensor_mul(out=gain[:], in0=rstd[:], in1=par[:, NB + k : NB + k + 1])
+            offset = small.tile([P, 1], F32)
+            nc.vector.scalar_tensor_tensor(
+                out=offset[:],
+                in0=mean_var[k][:, 0:1],
+                scalar=gain[:],
+                in1=par[:, 2 * NB + k : 2 * NB + k + 1],
+                op0=ALU.mult,
+                op1=ALU.subtract,
+            )
+            g, t = divmod(k, PACK)
+            nc.vector.tensor_scalar(
+                out=fused[:, g, :, t],
+                in0=act[k][:],
+                scalar1=gain[:],
+                scalar2=offset[:],
+                op0=ALU.mult,
+                op1=ALU.subtract,
+            )
+            if t == PACK - 1:
+                nc.vector.quantize_mx(
+                    out=f_codes[:, g, :].bitcast(FP8X4),
+                    scales=f_scales[:, g, :],
+                    in_=fused[:, g, :, :].rearrange("p r t -> p (r t)"),
+                )
+
+        norm_stages = (norm_relu, norm_stats, norm_sqrt, norm_apply)
+        for i in range(n_tiles + 2 + len(norm_stages)):
+            if i < n_tiles:
+                regroup(i)
+            if 1 <= i <= n_tiles:
+                quantise_and_multiply(i - 1)
+            for lag, stage in enumerate(norm_stages):
+                k, rest = divmod(i - 2 - lag, tiles_per_branch)
+                if rest == tiles_per_branch - 1 and 0 <= k < NB:
+                    stage(k)
+
+        out_ps = psum_misc.tile([P, DO], F32)
+        for g in range(2):
+            nc.tensor.matmul_mx(
+                out=out_ps[:],
+                lhsT=f_codes[:, g, :].bitcast(FP8X4),
+                lhsT_scale=f_scales[:, g, :],
+                rhs=wf_codes[:, g, :].bitcast(FP8X4),
+                rhs_scale=wf_scales[:, g, :],
+                start=(g == 0),
+                stop=(g == 1),
+            )
+        result = keep.tile([P, DO], F32)
+        nc.vector.tensor_tensor(out=result[:], in0=out_ps[:], in1=bias_out[:], op=ALU.add)
+        nc.vector.tensor_scalar_max(out=result[:], in0=result[:], scalar1=0.0)
+        nc.sync.dma_start(out=out, in_=result[:])

@@ -22,9 +22,10 @@ RUNS = 64
 CLASSES = 4
 ROWS = 16
 PASSES = ROWS // PACK
-TILE_COLS = ROWS * DO
+PLANE = ROWS * DO
+PAIR = 2
+PAIRS = HALVES * CLASSES // PAIR
 X_CHUNK = 4096
-LOAD_CLASSES = 2
 
 
 def tile_extremeoptimizationlayer_pa_k_kernel(tc, x, W, b, gamma, beta, Wf1, bf1, out):
@@ -40,14 +41,10 @@ def tile_extremeoptimizationlayer_pa_k_kernel(tc, x, W, b, gamma, beta, Wf1, bf1
         psum_x = ctx.enter_context(tc.psum_pool(name="psum_x", bufs=4))
         psum_acc = ctx.enter_context(tc.psum_pool(name="psum_acc", bufs=2))
         psum_misc = ctx.enter_context(tc.psum_pool(name="psum_misc", bufs=1))
+        ctx.enter_context(tc.manual_schedule())
 
         ident = keep.tile([P, P], F32)
         make_identity(nc, ident[:])
-
-        eps_col = keep.tile([P, 1], F32)
-        nc.vector.memset(eps_col[:], EPS)
-        warm = keep.tile([P, 1], F32)
-        nc.scalar.activation(out=warm[:], in_=eps_col[:], func=ACT.Sqrt)
 
         par_rows = keep.tile([P, P], BF16)
         nc.vector.memset(par_rows[:], 0.0)
@@ -59,53 +56,39 @@ def tile_extremeoptimizationlayer_pa_k_kernel(tc, x, W, b, gamma, beta, Wf1, bf1
         wf_raw = keep.tile([P, NB, DO], BF16)
         nc.scalar.dma_start(out=wf_raw[:], in_=Wf1.rearrange("(k p) n -> p k n", p=P))
 
+        eps_col = keep.tile([P, 1], F32)
+        nc.vector.memset(eps_col[:], EPS)
+        warm = keep.tile([P, 1], F32)
+        nc.scalar.activation(out=warm[:], in_=eps_col[:], func=ACT.Sqrt)
+
+        xs = keep.tile([P, HALVES, CLASSES, PLANE], BF16)
+        chunks_per_half = DI // HALVES // X_CHUNK
+        sorted_cols = X_CHUNK // CLASSES
+        x_chunks = {}
+
+        def load_x(a):
+            for j in range(a * chunks_per_half, (a + 1) * chunks_per_half):
+                x_chunks[j] = xin.tile([P, X_CHUNK], BF16, name="x_chunk")
+                nc.sync.dma_start(out=x_chunks[j][:], in_=x[:, j * X_CHUNK : (j + 1) * X_CHUNK])
+
+        def sort_by_class(a):
+            for j in range(chunks_per_half):
+                nc.vector.tensor_copy(
+                    out=xs[:, a, :, j * sorted_cols : (j + 1) * sorted_cols].rearrange(
+                        "r c (m e) -> r c m e", e=32
+                    ),
+                    in_=x_chunks[a * chunks_per_half + j][:].rearrange("r (m c e) -> r c m e", c=CLASSES, e=32),
+                )
+
+        load_x(0)
+        sort_by_class(0)
+
         par_f32 = keep.tile([P, P], F32)
         nc.vector.tensor_copy(out=par_f32[:], in_=par_rows[:])
         par_ps = psum_misc.tile([P, P], F32)
         nc.tensor.transpose(par_ps[:], par_f32[:], ident[:])
         par = keep.tile([P, 3 * NB], F32)
         nc.vector.tensor_copy(out=par[:], in_=par_ps[:, 0 : 3 * NB])
-
-        xs = keep.tile([P, HALVES, CLASSES, RUNS * 32], BF16)
-        chunks_per_half = DI // HALVES // X_CHUNK
-        runs_per_chunk = X_CHUNK // 128
-        for a in range(HALVES):
-            for j in range(chunks_per_half):
-                x_chunk = xin.tile([P, X_CHUNK], BF16)
-                first = (a * chunks_per_half + j) * X_CHUNK
-                nc.sync.dma_start(out=x_chunk[:], in_=x[:, first : first + X_CHUNK])
-                nc.vector.tensor_copy(
-                    out=xs[:, a, :, j * runs_per_chunk * 32 : (j + 1) * runs_per_chunk * 32].rearrange(
-                        "r c (m e) -> r c m e", e=32
-                    ),
-                    in_=x_chunk[:].rearrange("r (m c e) -> r c m e", c=CLASSES, e=32),
-                )
-
-        x_codes = keep.tile([P, HALVES * CLASSES * PASSES, B], U32, align_bytes=64)
-        x_scales = keep.tile([P, HALVES * CLASSES * PASSES, B], U8, align_bytes=64)
-        xs_words = xs[:].bitcast(F32)
-        for a in range(HALVES):
-            for c in range(CLASSES):
-                plane = xs_words[:, a, c, :].rearrange("r (p w) -> r p w", w=ROWS // 2)
-                xg = xgp.tile([P, PASSES, B, PACK], BF16, align_bytes=64)
-                xg_words = xg[:].bitcast(F32)
-                for pair in range(PASSES // 2):
-                    xt = psum_x.tile([P, 2, 2, B], F32)
-                    for s in range(2):
-                        for u in range(2):
-                            nc.tensor.transpose(
-                                xt[:, s, u, :], plane[:, :, 2 * (2 * pair + s) + u], ident[:]
-                            )
-                    nc.scalar.copy(
-                        out=xg_words[:, 2 * pair : 2 * pair + 2, :, :],
-                        in_=xt[:].rearrange("p s u r -> p s r u"),
-                    )
-                q0 = (a * CLASSES + c) * PASSES
-                nc.vector.quantize_mx(
-                    out=x_codes[:, q0 : q0 + PASSES, :].rearrange("p s r -> p (s r)").bitcast(FP8X4),
-                    scales=x_scales[:, q0 : q0 + PASSES, :].rearrange("p s r -> p (s r)"),
-                    in_=xg[:].rearrange("p s r t -> p (s r t)"),
-                )
 
         wf_grouped = keep.tile([P, 2, DO, PACK], BF16, align_bytes=64)
         nc.vector.tensor_copy(
@@ -119,18 +102,41 @@ def tile_extremeoptimizationlayer_pa_k_kernel(tc, x, W, b, gamma, beta, Wf1, bf1
             in_=wf_grouped[:].rearrange("p g n t -> p (g n t)"),
         )
 
+        x_codes = keep.tile([P, PAIRS, PAIR * PASSES, B], U32, align_bytes=64)
+        x_scales = keep.tile([P, PAIRS, PAIR * PASSES, B], U8, align_bytes=64)
+        xs_words = xs[:].bitcast(F32).rearrange("r a c (p w) -> r (a c) p w", w=ROWS // 2)
+        xg = {}
+
+        def transpose_x(pair):
+            xg[pair] = xgp.tile([P, PAIR * PASSES, B, PACK], BF16, align_bytes=64, name="xg")
+            xg_words = xg[pair][:].bitcast(F32)
+            for bank in range(PAIR * PASSES // 2):
+                xt = psum_x.tile([P, 2, 2, B], F32)
+                for s2 in range(2):
+                    c_in_pair, s = divmod(2 * bank + s2, PASSES)
+                    for u in range(2):
+                        nc.tensor.transpose(
+                            xt[:, s2, u, :], xs_words[:, pair * PAIR + c_in_pair, :, 2 * s + u], ident[:]
+                        )
+                nc.scalar.copy(
+                    out=xg_words[:, 2 * bank : 2 * bank + 2, :, :],
+                    in_=xt[:].rearrange("p s u r -> p s r u"),
+                )
+
+        def quantise_x(pair):
+            nc.vector.quantize_mx(
+                out=x_codes[:, pair, :, :].rearrange("p s r -> p (s r)").bitcast(FP8X4),
+                scales=x_scales[:, pair, :, :].rearrange("p s r -> p (s r)"),
+                in_=xg[pair][:].rearrange("p s r t -> p (s r t)"),
+            )
+
         w_loads = W.rearrange(
-            "k (a m l c h r) o -> k a l h m c (r o)", a=HALVES, m=RUNS, c=LOAD_CLASSES, h=2, r=ROWS
+            "k (a m l c h r) o -> k a l h m c (r o)", a=HALVES, m=RUNS, c=PAIR, h=2, r=ROWS
         )
         fused = keep.tile([P, 2, B, PACK], BF16, align_bytes=64)
         f_codes = keep.tile([P, 2, B], U32, align_bytes=64)
         f_scales = keep.tile([P, 2, B], U8, align_bytes=64)
-        half_cols = TILE_COLS // 2
-        pass_cols = TILE_COLS // PASSES
-        n_passes = HALVES * CLASSES * PASSES
-        tiles_per_branch = HALVES * CLASSES
-        n_tiles = NB * tiles_per_branch
-        loaded = {}
+        n_steps = NB * PAIRS
         grouped = {}
         acc = {}
         act = {}
@@ -138,43 +144,41 @@ def tile_extremeoptimizationlayer_pa_k_kernel(tc, x, W, b, gamma, beta, Wf1, bf1
         std = {}
 
         def regroup(i):
-            k, rest = divmod(i, tiles_per_branch)
-            a, c = divmod(rest, CLASSES)
-            load, c_in_load = divmod(c, LOAD_CLASSES)
-            if c_in_load == 0:
-                loaded[i // LOAD_CLASSES] = wraw.tile([P, LOAD_CLASSES, TILE_COLS], BF16, name="loaded")
-                for h in range(2):
-                    nc.sync.dma_start(out=loaded[i // LOAD_CLASSES][h:P:2, :, :], in_=w_loads[k, a, load, h])
-            raw = loaded[i // LOAD_CLASSES][:, c_in_load, :]
-            grouped[i] = wgrp.tile([P, TILE_COLS], BF16, align_bytes=64, name="grouped")
+            k, pair = divmod(i, PAIRS)
+            a, pair_in_half = divmod(pair, CLASSES // PAIR)
+            raw = wraw.tile([P, PAIR, PLANE], BF16)
+            for h in range(2):
+                nc.sync.dma_start(out=raw[h:P:2, :, :], in_=w_loads[k, a, pair_in_half, h])
+            grouped[i] = wgrp.tile([P, PAIR, PLANE], BF16, align_bytes=64, name="grouped")
             nc.vector.tensor_copy(
-                out=grouped[i][:, 0:half_cols].rearrange("p (s c i t) -> p s c t i", s=2, i=4, t=PACK),
-                in_=raw[:, 0:half_cols].rearrange("p (s t c i) -> p s c t i", s=2, i=4, t=PACK),
+                out=grouped[i][:, 0, :].rearrange("p (s c i t) -> p s c t i", s=PASSES, i=4, t=PACK),
+                in_=raw[:, 0, :].rearrange("p (s t c i) -> p s c t i", s=PASSES, i=4, t=PACK),
             )
-            for s in range(PASSES // 2, PASSES):
-                cols = slice(s * pass_cols, (s + 1) * pass_cols)
-                nc.scalar.copy(
-                    out=grouped[i][:, cols].rearrange("p (c i t) -> p c t i", i=4, t=PACK),
-                    in_=raw[:, cols].rearrange("p (t c i) -> p c t i", i=4, t=PACK),
-                )
+            nc.scalar.copy(
+                out=grouped[i][:, 1, :].rearrange("p (s o t) -> p s o t", s=PASSES, t=PACK),
+                in_=raw[:, 1, :].rearrange("p (s t o) -> p s o t", s=PASSES, t=PACK),
+            )
 
         def quantise_and_multiply(i):
-            k, rest = divmod(i, tiles_per_branch)
-            if rest == 0:
+            k, pair = divmod(i, PAIRS)
+            if pair == 0:
                 acc[k] = psum_acc.tile([P, B], F32, name="acc")
-            codes = wq.tile([P, PASSES * DO], U32, align_bytes=64)
-            scales = wq.tile([P, PASSES * DO], U8, align_bytes=64)
-            nc.vector.quantize_mx(out=codes[:].bitcast(FP8X4), scales=scales[:], in_=grouped[i][:])
-            for s in range(PASSES):
-                q = rest * PASSES + s
+            codes = wq.tile([P, PAIR * PASSES, DO], U32, align_bytes=64)
+            scales = wq.tile([P, PAIR * PASSES, DO], U8, align_bytes=64)
+            nc.vector.quantize_mx(
+                out=codes[:].rearrange("p s o -> p (s o)").bitcast(FP8X4),
+                scales=scales[:].rearrange("p s o -> p (s o)"),
+                in_=grouped[i][:].rearrange("p c e -> p (c e)"),
+            )
+            for s in range(PAIR * PASSES):
                 nc.tensor.matmul_mx(
                     out=acc[k][:],
-                    lhsT=codes[:, s * DO : (s + 1) * DO].bitcast(FP8X4),
-                    lhsT_scale=scales[:, s * DO : (s + 1) * DO],
-                    rhs=x_codes[:, q, :].bitcast(FP8X4),
-                    rhs_scale=x_scales[:, q, :],
-                    start=(q == 0),
-                    stop=(q == n_passes - 1),
+                    lhsT=codes[:, s, :].bitcast(FP8X4),
+                    lhsT_scale=scales[:, s, :],
+                    rhs=x_codes[:, pair, s, :].bitcast(FP8X4),
+                    rhs_scale=x_scales[:, pair, s, :],
+                    start=(pair == 0 and s == 0),
+                    stop=(pair == PAIRS - 1 and s == PAIR * PASSES - 1),
                 )
 
         def norm_relu(k):
@@ -222,14 +226,22 @@ def tile_extremeoptimizationlayer_pa_k_kernel(tc, x, W, b, gamma, beta, Wf1, bf1
                 )
 
         norm_stages = (norm_relu, norm_stats, norm_sqrt, norm_apply)
-        for i in range(n_tiles + 2 + len(norm_stages)):
-            if i < n_tiles:
+        for i in range(n_steps + 2 + len(norm_stages)):
+            if i < PAIRS:
+                transpose_x(i)
+            if i < n_steps:
                 regroup(i)
-            if 1 <= i <= n_tiles:
+            if i == 0:
+                load_x(1)
+            if i == 1:
+                sort_by_class(1)
+            if i < PAIRS:
+                quantise_x(i)
+            if 1 <= i <= n_steps:
                 quantise_and_multiply(i - 1)
             for lag, stage in enumerate(norm_stages):
-                k, rest = divmod(i - 2 - lag, tiles_per_branch)
-                if rest == tiles_per_branch - 1 and 0 <= k < NB:
+                k, pair = divmod(i - 2 - lag, PAIRS)
+                if pair == PAIRS - 1 and 0 <= k < NB:
                     stage(k)
 
         out_ps = psum_misc.tile([P, DO], F32)

@@ -26,6 +26,7 @@ PLANE = ROWS * DO
 PAIR = 2
 PAIRS = HALVES * CLASSES // PAIR
 X_CHUNK = 4096
+V_GROUPS = 15
 
 
 def tile_extremeoptimizationlayer_pa_k_kernel(tc, x, W, b, gamma, beta, Wf1, bf1, out):
@@ -33,7 +34,7 @@ def tile_extremeoptimizationlayer_pa_k_kernel(tc, x, W, b, gamma, beta, Wf1, bf1
     with ExitStack() as ctx:
         keep = ctx.enter_context(tc.tile_pool(name="keep", bufs=1))
         xin = ctx.enter_context(tc.tile_pool(name="xin", bufs=4))
-        xgp = ctx.enter_context(tc.tile_pool(name="xgp", bufs=2))
+        xgp = ctx.enter_context(tc.tile_pool(name="xgp", bufs=4))
         wraw = ctx.enter_context(tc.tile_pool(name="wraw", bufs=5))
         wgrp = ctx.enter_context(tc.tile_pool(name="wgrp", bufs=3))
         wq = ctx.enter_context(tc.tile_pool(name="wq", bufs=3))
@@ -58,18 +59,16 @@ def tile_extremeoptimizationlayer_pa_k_kernel(tc, x, W, b, gamma, beta, Wf1, bf1
 
         eps_col = keep.tile([P, 1], F32)
         nc.vector.memset(eps_col[:], EPS)
-        warm = keep.tile([P, 1], F32)
-        nc.scalar.activation(out=warm[:], in_=eps_col[:], func=ACT.Sqrt)
+        minus_half = keep.tile([P, 1], F32)
+        nc.vector.memset(minus_half[:], -0.5)
 
         xs = keep.tile([P, HALVES, CLASSES, PLANE], BF16)
         chunks_per_half = DI // HALVES // X_CHUNK
         sorted_cols = X_CHUNK // CLASSES
-        x_chunks = {}
-
-        def load_x(a):
-            for j in range(a * chunks_per_half, (a + 1) * chunks_per_half):
-                x_chunks[j] = xin.tile([P, X_CHUNK], BF16, name="x_chunk")
-                nc.sync.dma_start(out=x_chunks[j][:], in_=x[:, j * X_CHUNK : (j + 1) * X_CHUNK])
+        x_chunks = []
+        for j in range(DI // X_CHUNK):
+            x_chunks.append(xin.tile([P, X_CHUNK], BF16, name="x_chunk"))
+            nc.sync.dma_start(out=x_chunks[j][:], in_=x[:, j * X_CHUNK : (j + 1) * X_CHUNK])
 
         def sort_by_class(a):
             for j in range(chunks_per_half):
@@ -80,7 +79,6 @@ def tile_extremeoptimizationlayer_pa_k_kernel(tc, x, W, b, gamma, beta, Wf1, bf1
                     in_=x_chunks[a * chunks_per_half + j][:].rearrange("r (m c e) -> r c m e", c=CLASSES, e=32),
                 )
 
-        load_x(0)
         sort_by_class(0)
 
         par_f32 = keep.tile([P, P], F32)
@@ -102,14 +100,14 @@ def tile_extremeoptimizationlayer_pa_k_kernel(tc, x, W, b, gamma, beta, Wf1, bf1
             in_=wf_grouped[:].rearrange("p g n t -> p (g n t)"),
         )
 
+        sort_by_class(1)
+
         x_codes = keep.tile([P, PAIRS, PAIR * PASSES, B], U32, align_bytes=64)
         x_scales = keep.tile([P, PAIRS, PAIR * PASSES, B], U8, align_bytes=64)
         xs_words = xs[:].bitcast(F32).rearrange("r a c (p w) -> r (a c) p w", w=ROWS // 2)
-        xg = {}
-
-        def transpose_x(pair):
-            xg[pair] = xgp.tile([P, PAIR * PASSES, B, PACK], BF16, align_bytes=64, name="xg")
-            xg_words = xg[pair][:].bitcast(F32)
+        for pair in range(PAIRS):
+            xg = xgp.tile([P, PAIR * PASSES, B, PACK], BF16, align_bytes=64)
+            xg_words = xg[:].bitcast(F32)
             for bank in range(PAIR * PASSES // 2):
                 xt = psum_x.tile([P, 2, 2, B], F32)
                 for s2 in range(2):
@@ -122,12 +120,10 @@ def tile_extremeoptimizationlayer_pa_k_kernel(tc, x, W, b, gamma, beta, Wf1, bf1
                     out=xg_words[:, 2 * bank : 2 * bank + 2, :, :],
                     in_=xt[:].rearrange("p s u r -> p s r u"),
                 )
-
-        def quantise_x(pair):
             nc.vector.quantize_mx(
                 out=x_codes[:, pair, :, :].rearrange("p s r -> p (s r)").bitcast(FP8X4),
                 scales=x_scales[:, pair, :, :].rearrange("p s r -> p (s r)"),
-                in_=xg[pair][:].rearrange("p s r t -> p (s r t)"),
+                in_=xg[:].rearrange("p s r t -> p (s r t)"),
             )
 
         w_loads = W.rearrange(
@@ -141,7 +137,8 @@ def tile_extremeoptimizationlayer_pa_k_kernel(tc, x, W, b, gamma, beta, Wf1, bf1
         acc = {}
         act = {}
         mean_var = {}
-        std = {}
+        gain = {}
+        shift = {}
 
         def regroup(i):
             k, pair = divmod(i, PAIRS)
@@ -150,14 +147,11 @@ def tile_extremeoptimizationlayer_pa_k_kernel(tc, x, W, b, gamma, beta, Wf1, bf1
             for h in range(2):
                 nc.sync.dma_start(out=raw[h:P:2, :, :], in_=w_loads[k, a, pair_in_half, h])
             grouped[i] = wgrp.tile([P, PAIR, PLANE], BF16, align_bytes=64, name="grouped")
-            nc.vector.tensor_copy(
-                out=grouped[i][:, 0, :].rearrange("p (s c i t) -> p s c t i", s=PASSES, i=4, t=PACK),
-                in_=raw[:, 0, :].rearrange("p (s t c i) -> p s c t i", s=PASSES, i=4, t=PACK),
-            )
-            nc.scalar.copy(
-                out=grouped[i][:, 1, :].rearrange("p (s o t) -> p s o t", s=PASSES, t=PACK),
-                in_=raw[:, 1, :].rearrange("p (s t o) -> p s o t", s=PASSES, t=PACK),
-            )
+            src = raw[:].rearrange("p c (s t g i) -> p (c s) g t i", s=PASSES, t=PACK, i=4)
+            dst = grouped[i][:].rearrange("p c (s g i t) -> p (c s) g t i", s=PASSES, t=PACK, i=4)
+            nc.vector.tensor_copy(out=dst[:, :, 0:V_GROUPS], in_=src[:, :, 0:V_GROUPS])
+            for s in range(PAIR * PASSES):
+                nc.scalar.copy(out=dst[:, s, V_GROUPS:], in_=src[:, s, V_GROUPS:])
 
         def quantise_and_multiply(i):
             k, pair = divmod(i, PAIRS)
@@ -191,33 +185,28 @@ def tile_extremeoptimizationlayer_pa_k_kernel(tc, x, W, b, gamma, beta, Wf1, bf1
             mean_var[k] = small.tile([P, 2], F32, name="mean_var")
             nc.vector.bn_aggr(out=mean_var[k][:], in_=stats[:])
 
-        def norm_sqrt(k):
-            std[k] = small.tile([P, 1], F32, name="std")
-            nc.scalar.activation(out=std[k][:], in_=mean_var[k][:, 1:2], func=ACT.Sqrt, bias=eps_col[:])
+        def norm_factors(k):
+            var_eps = small.tile([P, 1], F32)
+            nc.gpsimd.tensor_tensor(out=var_eps[:], in0=mean_var[k][:, 1:2], in1=eps_col[:], op=ALU.add)
+            rstd = small.tile([P, 1], F32)
+            nc.gpsimd.tensor_tensor(out=rstd[:], in0=var_eps[:], in1=minus_half[:], op=ALU.pow)
+            gain[k] = small.tile([P, 1], F32, name="gain")
+            nc.gpsimd.tensor_tensor(out=gain[k][:], in0=rstd[:], in1=par[:, NB + k : NB + k + 1], op=ALU.mult)
+            mean_gain = small.tile([P, 1], F32)
+            nc.gpsimd.tensor_tensor(out=mean_gain[:], in0=mean_var[k][:, 0:1], in1=gain[k][:], op=ALU.mult)
+            shift[k] = small.tile([P, 1], F32, name="shift")
+            nc.gpsimd.tensor_tensor(
+                out=shift[k][:], in0=par[:, 2 * NB + k : 2 * NB + k + 1], in1=mean_gain[:], op=ALU.subtract
+            )
 
         def norm_apply(k):
-            rstd = small.tile([P, 1], F32)
-            nc.vector.reciprocal(out=rstd[:], in_=std[k][:])
-            gain = small.tile([P, 1], F32)
-            nc.vector.tensor_mul(out=gain[:], in0=rstd[:], in1=par[:, NB + k : NB + k + 1])
-            offset = small.tile([P, 1], F32)
-            nc.vector.scalar_tensor_tensor(
-                out=offset[:],
-                in0=mean_var[k][:, 0:1],
-                scalar=gain[:],
-                in1=par[:, 2 * NB + k : 2 * NB + k + 1],
-                op0=ALU.mult,
-                op1=ALU.subtract,
-            )
             g, t = divmod(k, PACK)
-            nc.vector.tensor_scalar(
-                out=fused[:, g, :, t],
-                in0=act[k][:],
-                scalar1=gain[:],
-                scalar2=offset[:],
-                op0=ALU.mult,
-                op1=ALU.subtract,
+            nc.scalar.activation(
+                out=fused[:, g, :, t], in_=act[k][:], func=ACT.Identity, scale=gain[k][:], bias=shift[k][:]
             )
+
+        def quantise_fused(k):
+            g, t = divmod(k, PACK)
             if t == PACK - 1:
                 nc.vector.quantize_mx(
                     out=f_codes[:, g, :].bitcast(FP8X4),
@@ -225,18 +214,10 @@ def tile_extremeoptimizationlayer_pa_k_kernel(tc, x, W, b, gamma, beta, Wf1, bf1
                     in_=fused[:, g, :, :].rearrange("p r t -> p (r t)"),
                 )
 
-        norm_stages = (norm_relu, norm_stats, norm_sqrt, norm_apply)
+        norm_stages = (norm_relu, norm_stats, norm_factors, norm_apply, quantise_fused)
         for i in range(n_steps + 2 + len(norm_stages)):
-            if i < PAIRS:
-                transpose_x(i)
             if i < n_steps:
                 regroup(i)
-            if i == 0:
-                load_x(1)
-            if i == 1:
-                sort_by_class(1)
-            if i < PAIRS:
-                quantise_x(i)
             if 1 <= i <= n_steps:
                 quantise_and_multiply(i - 1)
             for lag, stage in enumerate(norm_stages):

@@ -59,8 +59,8 @@ def tile_extremeoptimizationlayer_pa_k_kernel(tc, x, W, b, gamma, beta, Wf1, bf1
 
         eps_col = keep.tile([P, 1], F32)
         nc.vector.memset(eps_col[:], EPS)
-        minus_half = keep.tile([P, 1], F32)
-        nc.vector.memset(minus_half[:], -0.5)
+        warm = keep.tile([P, 1], F32)
+        nc.scalar.activation(out=warm[:], in_=eps_col[:], func=ACT.Sqrt)
 
         xs = keep.tile([P, HALVES, CLASSES, PLANE], BF16)
         chunks_per_half = DI // HALVES // X_CHUNK
@@ -137,8 +137,8 @@ def tile_extremeoptimizationlayer_pa_k_kernel(tc, x, W, b, gamma, beta, Wf1, bf1
         acc = {}
         act = {}
         mean_var = {}
-        gain = {}
-        shift = {}
+        std = {}
+        centred = {}
 
         def regroup(i):
             k, pair = divmod(i, PAIRS)
@@ -185,24 +185,31 @@ def tile_extremeoptimizationlayer_pa_k_kernel(tc, x, W, b, gamma, beta, Wf1, bf1
             mean_var[k] = small.tile([P, 2], F32, name="mean_var")
             nc.vector.bn_aggr(out=mean_var[k][:], in_=stats[:])
 
-        def norm_factors(k):
-            var_eps = small.tile([P, 1], F32)
-            nc.gpsimd.tensor_tensor(out=var_eps[:], in0=mean_var[k][:, 1:2], in1=eps_col[:], op=ALU.add)
+        def norm_sqrt(k):
+            std[k] = small.tile([P, 1], F32, name="std")
+            nc.scalar.activation(out=std[k][:], in_=mean_var[k][:, 1:2], func=ACT.Sqrt, bias=eps_col[:])
+
+        def norm_centre(k):
             rstd = small.tile([P, 1], F32)
-            nc.gpsimd.tensor_tensor(out=rstd[:], in0=var_eps[:], in1=minus_half[:], op=ALU.pow)
-            gain[k] = small.tile([P, 1], F32, name="gain")
-            nc.gpsimd.tensor_tensor(out=gain[k][:], in0=rstd[:], in1=par[:, NB + k : NB + k + 1], op=ALU.mult)
-            mean_gain = small.tile([P, 1], F32)
-            nc.gpsimd.tensor_tensor(out=mean_gain[:], in0=mean_var[k][:, 0:1], in1=gain[k][:], op=ALU.mult)
-            shift[k] = small.tile([P, 1], F32, name="shift")
-            nc.gpsimd.tensor_tensor(
-                out=shift[k][:], in0=par[:, 2 * NB + k : 2 * NB + k + 1], in1=mean_gain[:], op=ALU.subtract
+            nc.vector.reciprocal(out=rstd[:], in_=std[k][:])
+            centred[k] = small.tile([P, B], F32, name="centred")
+            nc.vector.tensor_scalar(
+                out=centred[k][:],
+                in0=act[k][:],
+                scalar1=mean_var[k][:, 0:1],
+                scalar2=rstd[:],
+                op0=ALU.subtract,
+                op1=ALU.mult,
             )
 
-        def norm_apply(k):
+        def norm_scale(k):
             g, t = divmod(k, PACK)
             nc.scalar.activation(
-                out=fused[:, g, :, t], in_=act[k][:], func=ACT.Identity, scale=gain[k][:], bias=shift[k][:]
+                out=fused[:, g, :, t],
+                in_=centred[k][:],
+                func=ACT.Identity,
+                scale=par[:, NB + k : NB + k + 1],
+                bias=par[:, 2 * NB + k : 2 * NB + k + 1],
             )
 
         def quantise_fused(k):
@@ -214,7 +221,7 @@ def tile_extremeoptimizationlayer_pa_k_kernel(tc, x, W, b, gamma, beta, Wf1, bf1
                     in_=fused[:, g, :, :].rearrange("p r t -> p (r t)"),
                 )
 
-        norm_stages = (norm_relu, norm_stats, norm_factors, norm_apply, quantise_fused)
+        norm_stages = (norm_relu, norm_stats, norm_sqrt, norm_centre, norm_scale, quantise_fused)
         for i in range(n_steps + 2 + len(norm_stages)):
             if i < n_steps:
                 regroup(i)

@@ -150,8 +150,7 @@ def tile_extremeoptimizationlayer_pa_k_kernel(tc, x, W, b, gamma, beta, Wf1, bf1
             src = raw[:].rearrange("p c (s t g i) -> p (c s) g t i", s=PASSES, t=PACK, i=4)
             dst = grouped[i][:].rearrange("p c (s g i t) -> p (c s) g t i", s=PASSES, t=PACK, i=4)
             nc.vector.tensor_copy(out=dst[:, :, 0:V_GROUPS], in_=src[:, :, 0:V_GROUPS])
-            for s in range(PAIR * PASSES):
-                nc.scalar.copy(out=dst[:, s, V_GROUPS:], in_=src[:, s, V_GROUPS:])
+            nc.scalar.copy(out=dst[:, :, V_GROUPS:], in_=src[:, :, V_GROUPS:])
 
         def quantise_and_multiply(i):
             k, pair = divmod(i, PAIRS)

@@ -52,8 +52,7 @@ def tile_extremeoptimizationlayer_pa_k_kernel(tc, x, W, b, gamma, beta, Wf1, bf1
         nc.scalar.dma_start(out=par_rows[0:NB, :], in_=b)
         nc.scalar.dma_start(out=par_rows[NB : 2 * NB, :], in_=gamma)
         nc.scalar.dma_start(out=par_rows[2 * NB : 3 * NB, :], in_=beta)
-        bias_out = keep.tile([P, DO], BF16)
-        nc.scalar.dma_start(out=bias_out[:], in_=bf1.partition_broadcast(P))
+        nc.scalar.dma_start(out=par_rows[3 * NB : 3 * NB + 1, :], in_=bf1.rearrange("(r n) -> r n", r=1))
         wf_raw = keep.tile([P, NB, DO], BF16)
         nc.scalar.dma_start(out=wf_raw[:], in_=Wf1.rearrange("(k p) n -> p k n", p=P))
 
@@ -83,10 +82,16 @@ def tile_extremeoptimizationlayer_pa_k_kernel(tc, x, W, b, gamma, beta, Wf1, bf1
 
         par_f32 = keep.tile([P, P], F32)
         nc.vector.tensor_copy(out=par_f32[:], in_=par_rows[:])
-        par_ps = psum_misc.tile([P, P], F32)
+        par_ps = psum_misc.tile([P, P], F32, name="square")
         nc.tensor.transpose(par_ps[:], par_f32[:], ident[:])
-        par = keep.tile([P, 3 * NB], F32)
-        nc.vector.tensor_copy(out=par[:], in_=par_ps[:, 0 : 3 * NB])
+        par = keep.tile([P, 3 * NB + 1], F32)
+        nc.vector.tensor_copy(out=par[:], in_=par_ps[:, 0 : 3 * NB + 1])
+        bias_ps = psum_misc.tile([P, DO], F32, name="square")
+        nc.tensor.matmul(
+            bias_ps[:], par[:, 3 * NB : 3 * NB + 1].to_broadcast([P, P]), ident[:], start=True, stop=True
+        )
+        bias_out = keep.tile([P, DO], F32)
+        nc.vector.tensor_copy(out=bias_out[:], in_=bias_ps[:])
 
         wf_grouped = keep.tile([P, 2, DO, PACK], BF16, align_bytes=64)
         nc.vector.tensor_copy(

@@ -34,10 +34,11 @@ def tile_extremeoptimizationlayer_pa_k_kernel(tc, x, W, b, gamma, beta, Wf1, bf1
     with ExitStack() as ctx:
         keep = ctx.enter_context(tc.tile_pool(name="keep", bufs=1))
         xin = ctx.enter_context(tc.tile_pool(name="xin", bufs=4))
-        xgp = ctx.enter_context(tc.tile_pool(name="xgp", bufs=4))
-        wraw = ctx.enter_context(tc.tile_pool(name="wraw", bufs=5))
+        xsp = ctx.enter_context(tc.tile_pool(name="xsp", bufs=HALVES))
+        xgp = ctx.enter_context(tc.tile_pool(name="xgp", bufs=2))
+        wraw = ctx.enter_context(tc.tile_pool(name="wraw", bufs=6))
         wgrp = ctx.enter_context(tc.tile_pool(name="wgrp", bufs=3))
-        wq = ctx.enter_context(tc.tile_pool(name="wq", bufs=3))
+        wq = ctx.enter_context(tc.tile_pool(name="wq", bufs=7))
         small = ctx.enter_context(tc.tile_pool(name="small", bufs=3))
         psum_x = ctx.enter_context(tc.psum_pool(name="psum_x", bufs=4))
         psum_acc = ctx.enter_context(tc.psum_pool(name="psum_acc", bufs=2))
@@ -61,84 +62,106 @@ def tile_extremeoptimizationlayer_pa_k_kernel(tc, x, W, b, gamma, beta, Wf1, bf1
         warm = keep.tile([P, 1], F32)
         nc.scalar.activation(out=warm[:], in_=eps_col[:], func=ACT.Sqrt)
 
-        xs = keep.tile([P, HALVES, CLASSES, PLANE], BF16)
-        chunks_per_half = DI // HALVES // X_CHUNK
-        sorted_cols = X_CHUNK // CLASSES
-        x_chunks = []
-        for j in range(DI // X_CHUNK):
-            x_chunks.append(xin.tile([P, X_CHUNK], BF16, name="x_chunk"))
+        w_loads = W.rearrange(
+            "k (a m l c h r) o -> k a l h m c (r o)", a=HALVES, m=RUNS, c=PAIR, h=2, r=ROWS
+        )
+        n_steps = NB * PAIRS
+        raw = {}
+        x_chunks = {}
+
+        def load_w(i):
+            k, pair = divmod(i, PAIRS)
+            a, pair_in_half = divmod(pair, CLASSES // PAIR)
+            raw[i] = wraw.tile([P, PAIR, PLANE], BF16, name="raw")
+            for h in range(2):
+                nc.sync.dma_start(out=raw[i][h:P:2, :, :], in_=w_loads[k, a, pair_in_half, h])
+
+        def load_x(j):
+            x_chunks[j] = xin.tile([P, X_CHUNK], BF16, name="x_chunk")
             nc.sync.dma_start(out=x_chunks[j][:], in_=x[:, j * X_CHUNK : (j + 1) * X_CHUNK])
 
-        def sort_by_class(a):
-            for j in range(chunks_per_half):
-                nc.vector.tensor_copy(
-                    out=xs[:, a, :, j * sorted_cols : (j + 1) * sorted_cols].rearrange(
-                        "r c (m e) -> r c m e", e=32
-                    ),
-                    in_=x_chunks[a * chunks_per_half + j][:].rearrange("r (m c e) -> r c m e", c=CLASSES, e=32),
-                )
+        load_w(0)
+        load_w(1)
+        for j in range(DI // X_CHUNK):
+            load_x(j)
+            load_w(2 + j)
+        early_loads = 2 + DI // X_CHUNK
 
-        sort_by_class(0)
-
-        par_f32 = keep.tile([P, P], F32)
-        nc.vector.tensor_copy(out=par_f32[:], in_=par_rows[:])
-        par_ps = psum_misc.tile([P, P], F32, name="square")
-        nc.tensor.transpose(par_ps[:], par_f32[:], ident[:])
-        par = keep.tile([P, 3 * NB + 1], F32)
-        nc.vector.tensor_copy(out=par[:], in_=par_ps[:, 0 : 3 * NB + 1])
-        bias_ps = psum_misc.tile([P, DO], F32, name="square")
-        nc.tensor.matmul(
-            bias_ps[:], par[:, 3 * NB : 3 * NB + 1].to_broadcast([P, P]), ident[:], start=True, stop=True
-        )
-        bias_out = keep.tile([P, DO], F32)
-        nc.vector.tensor_copy(out=bias_out[:], in_=bias_ps[:])
-
-        wf_grouped = keep.tile([P, 2, DO, PACK], BF16, align_bytes=64)
-        nc.vector.tensor_copy(
-            out=wf_grouped[:], in_=wf_raw[:].rearrange("p (g t) n -> p g n t", t=PACK)
-        )
-        wf_codes = keep.tile([P, 2, DO], U32, align_bytes=64)
-        wf_scales = keep.tile([P, 2, DO], U8, align_bytes=64)
-        nc.vector.quantize_mx(
-            out=wf_codes[:].rearrange("p g n -> p (g n)").bitcast(FP8X4),
-            scales=wf_scales[:].rearrange("p g n -> p (g n)"),
-            in_=wf_grouped[:].rearrange("p g n t -> p (g n t)"),
-        )
-
-        sort_by_class(1)
-
+        chunks_per_half = DI // HALVES // X_CHUNK
+        sorted_cols = X_CHUNK // CLASSES
+        xs = {}
+        x_grouped = {}
         x_codes = keep.tile([P, PAIRS, PAIR * PASSES, B], U32, align_bytes=64)
         x_scales = keep.tile([P, PAIRS, PAIR * PASSES, B], U8, align_bytes=64)
-        xs_words = xs[:].bitcast(F32).rearrange("r a c (p w) -> r (a c) p w", w=ROWS // 2)
-        for pair in range(PAIRS):
-            xg = xgp.tile([P, PAIR * PASSES, B, PACK], BF16, align_bytes=64)
-            xg_words = xg[:].bitcast(F32)
+
+        def x_sort(j):
+            a, part = divmod(j, chunks_per_half)
+            if part == 0:
+                xs[a] = xsp.tile([P, CLASSES, PLANE], BF16, name="xs")
+            nc.vector.tensor_copy(
+                out=xs[a][:, :, part * sorted_cols : (part + 1) * sorted_cols].rearrange(
+                    "r c (m e) -> r c m e", e=32
+                ),
+                in_=x_chunks[j][:].rearrange("r (m c e) -> r c m e", c=CLASSES, e=32),
+            )
+
+        def x_transpose(pair):
+            a, pair_in_half = divmod(pair, CLASSES // PAIR)
+            words = xs[a][:].bitcast(F32).rearrange("r c (p w) -> r c p w", w=ROWS // 2)
+            x_grouped[pair] = xgp.tile([P, PAIR * PASSES, B, PACK], BF16, align_bytes=64, name="x_grouped")
+            xg_words = x_grouped[pair][:].bitcast(F32)
             for bank in range(PAIR * PASSES // 2):
                 xt = psum_x.tile([P, 2, 2, B], F32)
                 for s2 in range(2):
                     c_in_pair, s = divmod(2 * bank + s2, PASSES)
                     for u in range(2):
                         nc.tensor.transpose(
-                            xt[:, s2, u, :], xs_words[:, pair * PAIR + c_in_pair, :, 2 * s + u], ident[:]
+                            xt[:, s2, u, :], words[:, pair_in_half * PAIR + c_in_pair, :, 2 * s + u], ident[:]
                         )
                 nc.scalar.copy(
                     out=xg_words[:, 2 * bank : 2 * bank + 2, :, :],
                     in_=xt[:].rearrange("p s u r -> p s r u"),
                 )
+
+        def x_quantise(pair):
             nc.vector.quantize_mx(
                 out=x_codes[:, pair, :, :].rearrange("p s r -> p (s r)").bitcast(FP8X4),
                 scales=x_scales[:, pair, :, :].rearrange("p s r -> p (s r)"),
-                in_=xg[:].rearrange("p s r t -> p (s r t)"),
+                in_=x_grouped[pair][:].rearrange("p s r t -> p (s r t)"),
             )
 
-        w_loads = W.rearrange(
-            "k (a m l c h r) o -> k a l h m c (r o)", a=HALVES, m=RUNS, c=PAIR, h=2, r=ROWS
-        )
+        def prepare_small_operands():
+            par_f32 = keep.tile([P, P], F32)
+            nc.vector.tensor_copy(out=par_f32[:], in_=par_rows[:])
+            par_ps = psum_misc.tile([P, P], F32, name="square")
+            nc.tensor.transpose(par_ps[:], par_f32[:], ident[:])
+            nc.vector.tensor_copy(out=par[:], in_=par_ps[:, 0 : 3 * NB + 1])
+            bias_ps = psum_misc.tile([P, DO], F32, name="square")
+            nc.tensor.matmul(
+                bias_ps[:], par[:, 3 * NB : 3 * NB + 1].to_broadcast([P, P]), ident[:], start=True, stop=True
+            )
+            nc.vector.tensor_copy(out=bias_out[:], in_=bias_ps[:])
+            wf_grouped = keep.tile([P, 2, DO, PACK], BF16, align_bytes=64)
+            nc.vector.tensor_copy(
+                out=wf_grouped[:], in_=wf_raw[:].rearrange("p (g t) n -> p g n t", t=PACK)
+            )
+            nc.vector.quantize_mx(
+                out=wf_codes[:].rearrange("p g n -> p (g n)").bitcast(FP8X4),
+                scales=wf_scales[:].rearrange("p g n -> p (g n)"),
+                in_=wf_grouped[:].rearrange("p g n t -> p (g n t)"),
+            )
+
+        par = keep.tile([P, 3 * NB + 1], F32)
+        bias_out = keep.tile([P, DO], F32)
+        wf_codes = keep.tile([P, 2, DO], U32, align_bytes=64)
+        wf_scales = keep.tile([P, 2, DO], U8, align_bytes=64)
+
         fused = keep.tile([P, 2, B, PACK], BF16, align_bytes=64)
         f_codes = keep.tile([P, 2, B], U32, align_bytes=64)
         f_scales = keep.tile([P, 2, B], U8, align_bytes=64)
-        n_steps = NB * PAIRS
         grouped = {}
+        codes = {}
+        scales = {}
         acc = {}
         act = {}
         mean_var = {}
@@ -146,33 +169,32 @@ def tile_extremeoptimizationlayer_pa_k_kernel(tc, x, W, b, gamma, beta, Wf1, bf1
         centred = {}
 
         def regroup(i):
-            k, pair = divmod(i, PAIRS)
-            a, pair_in_half = divmod(pair, CLASSES // PAIR)
-            raw = wraw.tile([P, PAIR, PLANE], BF16)
-            for h in range(2):
-                nc.sync.dma_start(out=raw[h:P:2, :, :], in_=w_loads[k, a, pair_in_half, h])
+            if i >= early_loads:
+                load_w(i)
             grouped[i] = wgrp.tile([P, PAIR, PLANE], BF16, align_bytes=64, name="grouped")
-            src = raw[:].rearrange("p c (s t g i) -> p (c s) g t i", s=PASSES, t=PACK, i=4)
+            src = raw[i][:].rearrange("p c (s t g i) -> p (c s) g t i", s=PASSES, t=PACK, i=4)
             dst = grouped[i][:].rearrange("p c (s g i t) -> p (c s) g t i", s=PASSES, t=PACK, i=4)
             nc.vector.tensor_copy(out=dst[:, :, 0:V_GROUPS], in_=src[:, :, 0:V_GROUPS])
             nc.scalar.copy(out=dst[:, :, V_GROUPS:], in_=src[:, :, V_GROUPS:])
 
-        def quantise_and_multiply(i):
+        def quantise(i):
+            codes[i] = wq.tile([P, PAIR * PASSES, DO], U32, align_bytes=64, name="codes")
+            scales[i] = wq.tile([P, PAIR * PASSES, DO], U8, align_bytes=64, name="scales")
+            nc.vector.quantize_mx(
+                out=codes[i][:].rearrange("p s o -> p (s o)").bitcast(FP8X4),
+                scales=scales[i][:].rearrange("p s o -> p (s o)"),
+                in_=grouped[i][:].rearrange("p c e -> p (c e)"),
+            )
+
+        def multiply(i):
             k, pair = divmod(i, PAIRS)
             if pair == 0:
                 acc[k] = psum_acc.tile([P, B], F32, name="acc")
-            codes = wq.tile([P, PAIR * PASSES, DO], U32, align_bytes=64)
-            scales = wq.tile([P, PAIR * PASSES, DO], U8, align_bytes=64)
-            nc.vector.quantize_mx(
-                out=codes[:].rearrange("p s o -> p (s o)").bitcast(FP8X4),
-                scales=scales[:].rearrange("p s o -> p (s o)"),
-                in_=grouped[i][:].rearrange("p c e -> p (c e)"),
-            )
             for s in range(PAIR * PASSES):
                 nc.tensor.matmul_mx(
                     out=acc[k][:],
-                    lhsT=codes[:, s, :].bitcast(FP8X4),
-                    lhsT_scale=scales[:, s, :],
+                    lhsT=codes[i][:, s, :].bitcast(FP8X4),
+                    lhsT_scale=scales[i][:, s, :],
                     rhs=x_codes[:, pair, s, :].bitcast(FP8X4),
                     rhs_scale=x_scales[:, pair, s, :],
                     start=(pair == 0 and s == 0),
@@ -225,16 +247,34 @@ def tile_extremeoptimizationlayer_pa_k_kernel(tc, x, W, b, gamma, beta, Wf1, bf1
                     in_=fused[:, g, :, :].rearrange("p r t -> p (r t)"),
                 )
 
+        x_sort_step = {1: 0, 2: 1, 4: 2, 5: 3}
+        x_pair_step = {3: 0, 4: 1, 6: 2, 7: 3}
         norm_stages = (norm_relu, norm_stats, norm_sqrt, norm_centre, norm_scale, quantise_fused)
+        stage_of = {}
+        multiplied = 0
         for i in range(n_steps + 2 + len(norm_stages)):
+            if i - 1 in x_pair_step:
+                x_quantise(x_pair_step[i - 1])
+            if i in x_pair_step:
+                x_transpose(x_pair_step[i])
             if i < n_steps:
                 regroup(i)
+            if i in x_sort_step:
+                x_sort(x_sort_step[i])
+            if i == 8:
+                prepare_small_operands()
             if 1 <= i <= n_steps:
-                quantise_and_multiply(i - 1)
-            for lag, stage in enumerate(norm_stages):
-                k, pair = divmod(i - 2 - lag, PAIRS)
-                if pair == PAIRS - 1 and 0 <= k < NB:
-                    stage(k)
+                quantise(i - 1)
+            for stage, k in stage_of.get(i, []):
+                stage(k)
+            x_ready = sum(1 for step in x_pair_step if step < i)
+            while multiplied < min(i, n_steps) and (x_ready == PAIRS or multiplied < x_ready):
+                multiply(multiplied)
+                k, pair = divmod(multiplied, PAIRS)
+                if pair == PAIRS - 1:
+                    for lag, stage in enumerate(norm_stages):
+                        stage_of.setdefault(i + 1 + lag, []).append((stage, k))
+                multiplied += 1
 
         out_ps = psum_misc.tile([P, DO], F32)
         for g in range(2):

@@ -27,18 +27,22 @@ PAIR = 2
 PAIRS = HALVES * CLASSES // PAIR
 X_CHUNK = 4096
 V_GROUPS = 15
+EARLY_V_GROUPS = 10
+EARLY = 4
+RAW_BUFS = 5
+X_BEFORE_PIECE = (4, 6, 8, 8)
 
 
 def tile_extremeoptimizationlayer_pa_k_kernel(tc, x, W, b, gamma, beta, Wf1, bf1, out):
     nc = tc.nc
     with ExitStack() as ctx:
         keep = ctx.enter_context(tc.tile_pool(name="keep", bufs=1))
-        xin = ctx.enter_context(tc.tile_pool(name="xin", bufs=4))
+        xin = ctx.enter_context(tc.tile_pool(name="xin", bufs=3))
         xsp = ctx.enter_context(tc.tile_pool(name="xsp", bufs=HALVES))
         xgp = ctx.enter_context(tc.tile_pool(name="xgp", bufs=2))
-        wraw = ctx.enter_context(tc.tile_pool(name="wraw", bufs=6))
+        wraw = ctx.enter_context(tc.tile_pool(name="wraw", bufs=RAW_BUFS))
         wgrp = ctx.enter_context(tc.tile_pool(name="wgrp", bufs=3))
-        wq = ctx.enter_context(tc.tile_pool(name="wq", bufs=7))
+        wq = ctx.enter_context(tc.tile_pool(name="wq", bufs=8))
         small = ctx.enter_context(tc.tile_pool(name="small", bufs=3))
         psum_x = ctx.enter_context(tc.psum_pool(name="psum_x", bufs=4))
         psum_acc = ctx.enter_context(tc.psum_pool(name="psum_acc", bufs=2))
@@ -60,32 +64,40 @@ def tile_extremeoptimizationlayer_pa_k_kernel(tc, x, W, b, gamma, beta, Wf1, bf1
         eps_col = keep.tile([P, 1], F32)
         nc.vector.memset(eps_col[:], EPS)
         warm = keep.tile([P, 1], F32)
-        nc.scalar.activation(out=warm[:], in_=eps_col[:], func=ACT.Sqrt)
+        nc.scalar.activation(out=warm[:], in_=eps_col[:], func=ACT.Abs_reciprocal_sqrt)
 
-        w_loads = W.rearrange(
-            "k (a m l c h r) o -> k a l h m c (r o)", a=HALVES, m=RUNS, c=PAIR, h=2, r=ROWS
-        )
-        n_steps = NB * PAIRS
+        pieces = []
+        for k in range(NB):
+            for pair in range(PAIRS):
+                if (k, pair) in ((0, 0), (NB - 1, PAIRS - 1)):
+                    pieces += [(k, pair, 0, 1), (k, pair, 1, 1)]
+                else:
+                    pieces.append((k, pair, 0, PAIR))
+        w_loads = W.rearrange("k (a m c h r) o -> k a h m c (r o)", a=HALVES, m=RUNS, c=CLASSES, h=2, r=ROWS)
         raw = {}
         x_chunks = {}
 
         def load_w(i):
-            k, pair = divmod(i, PAIRS)
+            k, pair, c0, n = pieces[i]
             a, pair_in_half = divmod(pair, CLASSES // PAIR)
-            raw[i] = wraw.tile([P, PAIR, PLANE], BF16, name="raw")
+            c0 += pair_in_half * PAIR
+            raw[i] = wraw.tile([P, n, PLANE], BF16, name="raw")
             for h in range(2):
-                nc.sync.dma_start(out=raw[i][h:P:2, :, :], in_=w_loads[k, a, pair_in_half, h])
+                nc.sync.dma_start(out=raw[i][h:P:2, :, :], in_=w_loads[k, a, h, :, c0 : c0 + n, :])
 
         def load_x(j):
             x_chunks[j] = xin.tile([P, X_CHUNK], BF16, name="x_chunk")
             nc.sync.dma_start(out=x_chunks[j][:], in_=x[:, j * X_CHUNK : (j + 1) * X_CHUNK])
 
-        load_w(0)
-        load_w(1)
-        for j in range(DI // X_CHUNK):
-            load_x(j)
-            load_w(2 + j)
-        early_loads = 2 + DI // X_CHUNK
+        def load(i):
+            for j, piece in enumerate(X_BEFORE_PIECE):
+                if piece == i:
+                    load_x(j)
+            if i < len(pieces):
+                load_w(i)
+
+        for i in range(RAW_BUFS):
+            load(i)
 
         chunks_per_half = DI // HALVES // X_CHUNK
         sorted_cols = X_CHUNK // CLASSES
@@ -164,22 +176,25 @@ def tile_extremeoptimizationlayer_pa_k_kernel(tc, x, W, b, gamma, beta, Wf1, bf1
         scales = {}
         acc = {}
         act = {}
+        stats = {}
         mean_var = {}
-        std = {}
+        rstd = {}
         centred = {}
 
         def regroup(i):
-            if i >= early_loads:
-                load_w(i)
-            grouped[i] = wgrp.tile([P, PAIR, PLANE], BF16, align_bytes=64, name="grouped")
+            n = pieces[i][3]
+            grouped[i] = wgrp.tile([P, n, PLANE], BF16, align_bytes=64, name="grouped")
             src = raw[i][:].rearrange("p c (s t g i) -> p (c s) g t i", s=PASSES, t=PACK, i=4)
             dst = grouped[i][:].rearrange("p c (s g i t) -> p (c s) g t i", s=PASSES, t=PACK, i=4)
-            nc.vector.tensor_copy(out=dst[:, :, 0:V_GROUPS], in_=src[:, :, 0:V_GROUPS])
-            nc.scalar.copy(out=dst[:, :, V_GROUPS:], in_=src[:, :, V_GROUPS:])
+            split = EARLY_V_GROUPS if i < EARLY else V_GROUPS
+            nc.vector.tensor_copy(out=dst[:, :, 0:split], in_=src[:, :, 0:split])
+            nc.scalar.copy(out=dst[:, :, split:], in_=src[:, :, split:])
+            load(i + RAW_BUFS)
 
         def quantise(i):
-            codes[i] = wq.tile([P, PAIR * PASSES, DO], U32, align_bytes=64, name="codes")
-            scales[i] = wq.tile([P, PAIR * PASSES, DO], U8, align_bytes=64, name="scales")
+            n = pieces[i][3]
+            codes[i] = wq.tile([P, n * PASSES, DO], U32, align_bytes=64, name="codes")
+            scales[i] = wq.tile([P, n * PASSES, DO], U8, align_bytes=64, name="scales")
             nc.vector.quantize_mx(
                 out=codes[i][:].rearrange("p s o -> p (s o)").bitcast(FP8X4),
                 scales=scales[i][:].rearrange("p s o -> p (s o)"),
@@ -187,18 +202,19 @@ def tile_extremeoptimizationlayer_pa_k_kernel(tc, x, W, b, gamma, beta, Wf1, bf1
             )
 
         def multiply(i):
-            k, pair = divmod(i, PAIRS)
-            if pair == 0:
+            k, pair, c0, n = pieces[i]
+            if pair == 0 and c0 == 0:
                 acc[k] = psum_acc.tile([P, B], F32, name="acc")
-            for s in range(PAIR * PASSES):
+            for s in range(n * PASSES):
+                x_pass = c0 * PASSES + s
                 nc.tensor.matmul_mx(
                     out=acc[k][:],
                     lhsT=codes[i][:, s, :].bitcast(FP8X4),
                     lhsT_scale=scales[i][:, s, :],
-                    rhs=x_codes[:, pair, s, :].bitcast(FP8X4),
-                    rhs_scale=x_scales[:, pair, s, :],
-                    start=(pair == 0 and s == 0),
-                    stop=(pair == PAIRS - 1 and s == PAIR * PASSES - 1),
+                    rhs=x_codes[:, pair, x_pass, :].bitcast(FP8X4),
+                    rhs_scale=x_scales[:, pair, x_pass, :],
+                    start=(pair == 0 and x_pass == 0),
+                    stop=(pair == PAIRS - 1 and x_pass == PAIR * PASSES - 1),
                 )
 
         def norm_relu(k):
@@ -206,24 +222,26 @@ def tile_extremeoptimizationlayer_pa_k_kernel(tc, x, W, b, gamma, beta, Wf1, bf1
             nc.scalar.activation(out=act[k][:], in_=acc[k][:], func=ACT.Relu, bias=par[:, k : k + 1])
 
         def norm_stats(k):
-            stats = small.tile([P, 6], F32)
-            nc.vector.bn_stats(out=stats[:], in_=act[k][:])
-            mean_var[k] = small.tile([P, 2], F32, name="mean_var")
-            nc.vector.bn_aggr(out=mean_var[k][:], in_=stats[:])
+            stats[k] = small.tile([P, 6], F32, name="stats")
+            nc.vector.bn_stats(out=stats[k][:], in_=act[k][:])
 
-        def norm_sqrt(k):
-            std[k] = small.tile([P, 1], F32, name="std")
-            nc.scalar.activation(out=std[k][:], in_=mean_var[k][:, 1:2], func=ACT.Sqrt, bias=eps_col[:])
+        def norm_aggregate(k):
+            mean_var[k] = small.tile([P, 2], F32, name="mean_var")
+            nc.vector.bn_aggr(out=mean_var[k][:], in_=stats[k][:])
+
+        def norm_rstd(k):
+            rstd[k] = small.tile([P, 1], F32, name="rstd")
+            nc.scalar.activation(
+                out=rstd[k][:], in_=mean_var[k][:, 1:2], func=ACT.Abs_reciprocal_sqrt, bias=eps_col[:]
+            )
 
         def norm_centre(k):
-            rstd = small.tile([P, 1], F32)
-            nc.vector.reciprocal(out=rstd[:], in_=std[k][:])
             centred[k] = small.tile([P, B], F32, name="centred")
             nc.vector.tensor_scalar(
                 out=centred[k][:],
                 in0=act[k][:],
                 scalar1=mean_var[k][:, 0:1],
-                scalar2=rstd[:],
+                scalar2=rstd[k][:],
                 op0=ALU.subtract,
                 op1=ALU.mult,
             )
@@ -247,34 +265,50 @@ def tile_extremeoptimizationlayer_pa_k_kernel(tc, x, W, b, gamma, beta, Wf1, bf1
                     in_=fused[:, g, :, :].rearrange("p r t -> p (r t)"),
                 )
 
-        x_sort_step = {1: 0, 2: 1, 4: 2, 5: 3}
-        x_pair_step = {3: 0, 4: 1, 6: 2, 7: 3}
-        norm_stages = (norm_relu, norm_stats, norm_sqrt, norm_centre, norm_scale, quantise_fused)
-        stage_of = {}
+        sort_step = {0: 3, 1: 5, 2: 7, 3: 7}
+        pair_step = {0: 6, 1: 7, 2: 8, 3: 9}
+        small_operands_step = 2
+        norm_stages = (
+            (2, "before", norm_relu),
+            (3, "behind", norm_stats),
+            (4, "before", norm_aggregate),
+            (5, "behind", norm_rstd),
+            (6, "before", norm_centre),
+            (7, "behind", norm_scale),
+            (8, "before", quantise_fused),
+        )
+        due = {}
         multiplied = 0
-        for i in range(n_steps + 2 + len(norm_stages)):
-            if i - 1 in x_pair_step:
-                x_quantise(x_pair_step[i - 1])
-            if i in x_pair_step:
-                x_transpose(x_pair_step[i])
-            if i < n_steps:
-                regroup(i)
-            if i in x_sort_step:
-                x_sort(x_sort_step[i])
-            if i == 8:
-                prepare_small_operands()
-            if 1 <= i <= n_steps:
-                quantise(i - 1)
-            for stage, k in stage_of.get(i, []):
+        for i in range(len(pieces) + 1):
+            for q in range(PAIRS):
+                if pair_step[q] + 1 == i:
+                    x_quantise(q)
+                if pair_step[q] == i:
+                    x_transpose(q)
+            for stage, k in due.get((i, "before"), []):
                 stage(k)
-            x_ready = sum(1 for step in x_pair_step if step < i)
-            while multiplied < min(i, n_steps) and (x_ready == PAIRS or multiplied < x_ready):
+            if i < len(pieces):
+                regroup(i)
+            for j in sort_step:
+                if sort_step[j] == i:
+                    x_sort(j)
+            for stage, k in due.get((i, "behind"), []):
+                stage(k)
+            if i == small_operands_step:
+                prepare_small_operands()
+            if i >= 1:
+                quantise(i - 1)
+            while multiplied < i and pair_step[pieces[multiplied][1]] < i:
                 multiply(multiplied)
-                k, pair = divmod(multiplied, PAIRS)
-                if pair == PAIRS - 1:
-                    for lag, stage in enumerate(norm_stages):
-                        stage_of.setdefault(i + 1 + lag, []).append((stage, k))
+                k, pair, c0, n = pieces[multiplied]
                 multiplied += 1
+                if pair == PAIRS - 1 and c0 + n == PAIR:
+                    for lag, place, stage in norm_stages:
+                        due.setdefault((i + lag, place), []).append((stage, k))
+        for step in range(len(pieces) + 1, len(pieces) + 10):
+            for place in ("before", "behind"):
+                for stage, k in due.get((step, place), []):
+                    stage(k)
 
         out_ps = psum_misc.tile([P, DO], F32)
         for g in range(2):

@@ -26,8 +26,9 @@ PLANE = ROWS * DO
 PAIR = 2
 PAIRS = HALVES * CLASSES // PAIR
 X_CHUNK = 4096
-V_GROUPS = 15
-EARLY_V_GROUPS = 10
+RUN = 8
+V_GROUPS = 8
+EARLY_V_GROUPS = 5
 EARLY = 4
 RAW_BUFS = 5
 X_BEFORE_PIECE = (4, 6, 8, 8)
@@ -184,8 +185,8 @@ def tile_extremeoptimizationlayer_pa_k_kernel(tc, x, W, b, gamma, beta, Wf1, bf1
         def regroup(i):
             n = pieces[i][3]
             grouped[i] = wgrp.tile([P, n, PLANE], BF16, align_bytes=64, name="grouped")
-            src = raw[i][:].rearrange("p c (s t g i) -> p (c s) g t i", s=PASSES, t=PACK, i=4)
-            dst = grouped[i][:].rearrange("p c (s g i t) -> p (c s) g t i", s=PASSES, t=PACK, i=4)
+            src = raw[i][:].rearrange("p c (s t g i) -> p (c s) g t i", s=PASSES, t=PACK, i=RUN)
+            dst = grouped[i][:].rearrange("p c (s g i t) -> p (c s) g t i", s=PASSES, t=PACK, i=RUN)
             split = EARLY_V_GROUPS if i < EARLY else V_GROUPS
             nc.vector.tensor_copy(out=dst[:, :, 0:split], in_=src[:, :, 0:split])
             nc.scalar.copy(out=dst[:, :, split:], in_=src[:, :, split:])

from contextlib import ExitStack

import concourse.mybir as mybir
from concourse.masks import make_identity

F32 = mybir.dt.float32
BF16 = mybir.dt.bfloat16
U32 = mybir.dt.uint32
U8 = mybir.dt.uint8
FP8X4 = mybir.dt.float8_e4m3fn_x4
ACT = mybir.ActivationFunctionType
ALU = mybir.AluOpType

P = 128
PACK = 4
NB, DI, DO, B = 8, 16384, 128, 128
EPS = 1e-5
FLOPS = 2 * B * DI * NB * DO + 2 * B * NB * DO * DO

HALVES = 2
RUNS = 64
CLASSES = 4
ROWS = 16
PASSES = ROWS // PACK
PLANE = ROWS * DO
PAIR = 2
PAIRS = HALVES * CLASSES // PAIR
X_CHUNK = 4096
RUN = 8
V_GROUPS = 8
EARLY_V_GROUPS = 5
EARLY = 4
RAW_BUFS = 5
X_BEFORE_PIECE = (4, 6, 8, 8)


def tile_extremeoptimizationlayer_pa_k_kernel(tc, x, W, b, gamma, beta, Wf1, bf1, out):
    nc = tc.nc
    with ExitStack() as ctx:
        keep = ctx.enter_context(tc.tile_pool(name="keep", bufs=1))
        xin = ctx.enter_context(tc.tile_pool(name="xin", bufs=3))
        xsp = ctx.enter_context(tc.tile_pool(name="xsp", bufs=HALVES))
        xgp = ctx.enter_context(tc.tile_pool(name="xgp", bufs=2))
        wraw = ctx.enter_context(tc.tile_pool(name="wraw", bufs=RAW_BUFS))
        wgrp = ctx.enter_context(tc.tile_pool(name="wgrp", bufs=3))
        wq = ctx.enter_context(tc.tile_pool(name="wq", bufs=8))
        small = ctx.enter_context(tc.tile_pool(name="small", bufs=3))
        psum_x = ctx.enter_context(tc.psum_pool(name="psum_x", bufs=4))
        psum_acc = ctx.enter_context(tc.psum_pool(name="psum_acc", bufs=2))
        psum_misc = ctx.enter_context(tc.psum_pool(name="psum_misc", bufs=1))
        ctx.enter_context(tc.manual_schedule())

        ident = keep.tile([P, P], F32)
        make_identity(nc, ident[:])

        par_rows = keep.tile([P, P], BF16)
        nc.vector.memset(par_rows[:], 0.0)
        nc.scalar.dma_start(out=par_rows[0:NB, :], in_=b)
        nc.scalar.dma_start(out=par_rows[NB : 2 * NB, :], in_=gamma)
        nc.scalar.dma_start(out=par_rows[2 * NB : 3 * NB, :], in_=beta)
        nc.scalar.dma_start(out=par_rows[3 * NB : 3 * NB + 1, :], in_=bf1.rearrange("(r n) -> r n", r=1))
        wf_raw = keep.tile([P, NB, DO], BF16)
        nc.scalar.dma_start(out=wf_raw[:], in_=Wf1.rearrange("(k p) n -> p k n", p=P))

        eps_col = keep.tile([P, 1], F32)
        nc.vector.memset(eps_col[:], EPS)
        warm = keep.tile([P, 1], F32)
        nc.scalar.activation(out=warm[:], in_=eps_col[:], func=ACT.Abs_reciprocal_sqrt)

        pieces = []
        for k in range(NB):
            for pair in range(PAIRS):
                if (k, pair) in ((0, 0), (NB - 1, PAIRS - 1)):
                    pieces += [(k, pair, 0, 1), (k, pair, 1, 1)]
                else:
                    pieces.append((k, pair, 0, PAIR))
        w_loads = W.rearrange("k (a m c h r) o -> k a h m c (r o)", a=HALVES, m=RUNS, c=CLASSES, h=2, r=ROWS)
        raw = {}
        x_chunks = {}

        def load_w(i):
            k, pair, c0, n = pieces[i]
            a, pair_in_half = divmod(pair, CLASSES // PAIR)
            c0 += pair_in_half * PAIR
            raw[i] = wraw.tile([P, n, PLANE], BF16, name="raw")
            for h in range(2):
                nc.sync.dma_start(out=raw[i][h:P:2, :, :], in_=w_loads[k, a, h, :, c0 : c0 + n, :])

        def load_x(j):
            x_chunks[j] = xin.tile([P, X_CHUNK], BF16, name="x_chunk")
            nc.sync.dma_start(out=x_chunks[j][:], in_=x[:, j * X_CHUNK : (j + 1) * X_CHUNK])

        def load(i):
            for j, piece in enumerate(X_BEFORE_PIECE):
                if piece == i:
                    load_x(j)
            if i < len(pieces):
                load_w(i)

        for i in range(RAW_BUFS):
            load(i)

        chunks_per_half = DI // HALVES // X_CHUNK
        sorted_cols = X_CHUNK // CLASSES
        xs = {}
        x_grouped = {}
        x_codes = keep.tile([P, PAIRS, PAIR * PASSES, B], U32, align_bytes=64)
        x_scales = keep.tile([P, PAIRS, PAIR * PASSES, B], U8, align_bytes=64)

        def x_sort(j):
            a, part = divmod(j, chunks_per_half)
            if part == 0:
                xs[a] = xsp.tile([P, CLASSES, PLANE], BF16, name="xs")
            nc.vector.tensor_copy(
                out=xs[a][:, :, part * sorted_cols : (part + 1) * sorted_cols].rearrange(
                    "r c (m e) -> r c m e", e=32
                ),
                in_=x_chunks[j][:].rearrange("r (m c e) -> r c m e", c=CLASSES, e=32),
            )

        def x_transpose(pair):
            a, pair_in_half = divmod(pair, CLASSES // PAIR)
            words = xs[a][:].bitcast(F32).rearrange("r c (p w) -> r c p w", w=ROWS // 2)
            x_grouped[pair] = xgp.tile([P, PAIR * PASSES, B, PACK], BF16, align_bytes=64, name="x_grouped")
            xg_words = x_grouped[pair][:].bitcast(F32)
            for bank in range(PAIR * PASSES // 2):
                xt = psum_x.tile([P, 2, 2, B], F32)
                for s2 in range(2):
                    c_in_pair, s = divmod(2 * bank + s2, PASSES)
                    for u in range(2):
                        nc.tensor.transpose(
                            xt[:, s2, u, :], words[:, pair_in_half * PAIR + c_in_pair, :, 2 * s + u], ident[:]
                        )
                nc.scalar.copy(
                    out=xg_words[:, 2 * bank : 2 * bank + 2, :, :],
                    in_=xt[:].rearrange("p s u r -> p s r u"),
                )

        def x_quantise(pair):
            nc.vector.quantize_mx(
                out=x_codes[:, pair, :, :].rearrange("p s r -> p (s r)").bitcast(FP8X4),
                scales=x_scales[:, pair, :, :].rearrange("p s r -> p (s r)"),
                in_=x_grouped[pair][:].rearrange("p s r t -> p (s r t)"),
            )

        def prepare_small_operands():
            par_f32 = keep.tile([P, P], F32)
            nc.vector.tensor_copy(out=par_f32[:], in_=par_rows[:])
            par_ps = psum_misc.tile([P, P], F32, name="square")
            nc.tensor.transpose(par_ps[:], par_f32[:], ident[:])
            nc.vector.tensor_copy(out=par[:], in_=par_ps[:, 0 : 3 * NB + 1])
            bias_ps = psum_misc.tile([P, DO], F32, name="square")
            nc.tensor.matmul(
                bias_ps[:], par[:, 3 * NB : 3 * NB + 1].to_broadcast([P, P]), ident[:], start=True, stop=True
            )
            nc.vector.tensor_copy(out=bias_out[:], in_=bias_ps[:])
            wf_grouped = keep.tile([P, 2, DO, PACK], BF16, align_bytes=64)
            nc.vector.tensor_copy(
                out=wf_grouped[:], in_=wf_raw[:].rearrange("p (g t) n -> p g n t", t=PACK)
            )
            nc.vector.quantize_mx(
                out=wf_codes[:].rearrange("p g n -> p (g n)").bitcast(FP8X4),
                scales=wf_scales[:].rearrange("p g n -> p (g n)"),
                in_=wf_grouped[:].rearrange("p g n t -> p (g n t)"),
            )

        par = keep.tile([P, 3 * NB + 1], F32)
        bias_out = keep.tile([P, DO], F32)
        wf_codes = keep.tile([P, 2, DO], U32, align_bytes=64)
        wf_scales = keep.tile([P, 2, DO], U8, align_bytes=64)

        fused = keep.tile([P, 2, B, PACK], BF16, align_bytes=64)
        f_codes = keep.tile([P, 2, B], U32, align_bytes=64)
        f_scales = keep.tile([P, 2, B], U8, align_bytes=64)
        grouped = {}
        codes = {}
        scales = {}
        acc = {}
        act = {}
        stats = {}
        mean_var = {}
        rstd = {}
        centred = {}

        def regroup(i):
            n = pieces[i][3]
            grouped[i] = wgrp.tile([P, n, PLANE], BF16, align_bytes=64, name="grouped")
            src = raw[i][:].rearrange("p c (s t g i) -> p (c s) g t i", s=PASSES, t=PACK, i=RUN)
            dst = grouped[i][:].rearrange("p c (s g i t) -> p (c s) g t i", s=PASSES, t=PACK, i=RUN)
            split = EARLY_V_GROUPS if i < EARLY else V_GROUPS
            nc.vector.tensor_copy(out=dst[:, :, 0:split], in_=src[:, :, 0:split])
            nc.scalar.copy(out=dst[:, :, split:], in_=src[:, :, split:])
            load(i + RAW_BUFS)

        def quantise(i):
            n = pieces[i][3]
            codes[i] = wq.tile([P, n * PASSES, DO], U32, align_bytes=64, name="codes")
            scales[i] = wq.tile([P, n * PASSES, DO], U8, align_bytes=64, name="scales")
            nc.vector.quantize_mx(
                out=codes[i][:].rearrange("p s o -> p (s o)").bitcast(FP8X4),
                scales=scales[i][:].rearrange("p s o -> p (s o)"),
                in_=grouped[i][:].rearrange("p c e -> p (c e)"),
            )

        def multiply(i):
            k, pair, c0, n = pieces[i]
            if pair == 0 and c0 == 0:
                acc[k] = psum_acc.tile([P, B], F32, name="acc")
            for s in range(n * PASSES):
                x_pass = c0 * PASSES + s
                nc.tensor.matmul_mx(
                    out=acc[k][:],
                    lhsT=codes[i][:, s, :].bitcast(FP8X4),
                    lhsT_scale=scales[i][:, s, :],
                    rhs=x_codes[:, pair, x_pass, :].bitcast(FP8X4),
                    rhs_scale=x_scales[:, pair, x_pass, :],
                    start=(pair == 0 and x_pass == 0),
                    stop=(pair == PAIRS - 1 and x_pass == PAIR * PASSES - 1),
                )

        def norm_relu(k):
            act[k] = small.tile([P, B], F32, name="act")
            nc.scalar.activation(out=act[k][:], in_=acc[k][:], func=ACT.Relu, bias=par[:, k : k + 1])

        def norm_stats(k):
            stats[k] = small.tile([P, 6], F32, name="stats")
            nc.vector.bn_stats(out=stats[k][:], in_=act[k][:])

        def norm_aggregate(k):
            mean_var[k] = small.tile([P, 2], F32, name="mean_var")
            nc.vector.bn_aggr(out=mean_var[k][:], in_=stats[k][:])

        def norm_rstd(k):
            rstd[k] = small.tile([P, 1], F32, name="rstd")
            nc.scalar.activation(
                out=rstd[k][:], in_=mean_var[k][:, 1:2], func=ACT.Abs_reciprocal_sqrt, bias=eps_col[:]
            )

        def norm_centre(k):
            centred[k] = small.tile([P, B], F32, name="centred")
            nc.vector.tensor_scalar(
                out=centred[k][:],
                in0=act[k][:],
                scalar1=mean_var[k][:, 0:1],
                scalar2=rstd[k][:],
                op0=ALU.subtract,
                op1=ALU.mult,
            )

        def norm_scale(k):
            g, t = divmod(k, PACK)
            nc.scalar.activation(
                out=fused[:, g, :, t],
                in_=centred[k][:],
                func=ACT.Identity,
                scale=par[:, NB + k : NB + k + 1],
                bias=par[:, 2 * NB + k : 2 * NB + k + 1],
            )

        def quantise_fused(k):
            g, t = divmod(k, PACK)
            if t == PACK - 1:
                nc.vector.quantize_mx(
                    out=f_codes[:, g, :].bitcast(FP8X4),
                    scales=f_scales[:, g, :],
                    in_=fused[:, g, :, :].rearrange("p r t -> p (r t)"),
                )

        sort_step = {0: 3, 1: 5, 2: 7, 3: 7}
        pair_step = {0: 6, 1: 7, 2: 8, 3: 9}
        small_operands_step = 2
        norm_stages = (
            (2, "before", norm_relu),
            (3, "behind", norm_stats),
            (4, "before", norm_aggregate),
            (5, "behind", norm_rstd),
            (6, "before", norm_centre),
            (7, "behind", norm_scale),
            (8, "before", quantise_fused),
        )
        due = {}
        multiplied = 0
        for i in range(len(pieces) + 1):
            for q in range(PAIRS):
                if pair_step[q] + 1 == i:
                    x_quantise(q)
                if pair_step[q] == i:
                    x_transpose(q)
            for stage, k in due.get((i, "before"), []):
                stage(k)
            if i < len(pieces):
                regroup(i)
            for j in sort_step:
                if sort_step[j] == i:
                    x_sort(j)
            for stage, k in due.get((i, "behind"), []):
                stage(k)
            if i == small_operands_step:
                prepare_small_operands()
            if i >= 1:
                quantise(i - 1)
            while multiplied < i and pair_step[pieces[multiplied][1]] < i:
                multiply(multiplied)
                k, pair, c0, n = pieces[multiplied]
                multiplied += 1
                if pair == PAIRS - 1 and c0 + n == PAIR:
                    for lag, place, stage in norm_stages:
                        due.setdefault((i + lag, place), []).append((stage, k))
        for step in range(len(pieces) + 1, len(pieces) + 10):
            for place in ("before", "behind"):
                for stage, k in due.get((step, place), []):
                    stage(k)

        out_ps = psum_misc.tile([P, DO], F32)
        for g in range(2):
            nc.tensor.matmul_mx(
                out=out_ps[:],
                lhsT=f_codes[:, g, :].bitcast(FP8X4),
                lhsT_scale=f_scales[:, g, :],
                rhs=wf_codes[:, g, :].bitcast(FP8X4),
                rhs_scale=wf_scales[:, g, :],
                start=(g == 0),
                stop=(g == 1),
            )
        result = keep.tile([P, DO], F32)
        nc.vector.tensor_tensor(out=result[:], in0=out_ps[:], in1=bias_out[:], op=ALU.add)
        nc.vector.tensor_scalar_max(out=result[:], in0=result[:], scalar1=0.0)
        nc.sync.dma_start(out=out, in_=result[:])
